import numpy as np
import ml_dtypes


def mxq(x, axis, fmt="e4m3"):
    dtype, down = {"e4m3": (ml_dtypes.float8_e4m3fn, 7), "e5m2": (ml_dtypes.float8_e5m2, 14)}[fmt]
    v = np.moveaxis(np.asarray(x, np.float32).astype(ml_dtypes.bfloat16).astype(np.float64), axis, -1)
    blocks = v.reshape(v.shape[:-1] + (-1, 32))
    amax = np.abs(blocks).max(-1, keepdims=True)
    byte = np.maximum(np.where(amax > 0, np.frexp(amax)[1] - 1 + 127, 0) - down, 1)
    scale = np.exp2(byte - 127.0)
    codes = (blocks / scale).astype(np.float32).astype(dtype).astype(np.float64)
    return np.moveaxis((codes * scale).reshape(v.shape), -1, axis)


WIDE = False


def mx_kscale(k):
    if not WIDE:
        return np.ones(k)
    levels = np.array([10, -10, 5, -5, 0])
    a = np.random.permutation(np.resize(levels, k // 512 * 4)).reshape(k // 512, 4)
    idx = np.arange(k)
    return np.exp2(a[idx // 512, idx % 128 // 32])


BF16 = ml_dtypes.bfloat16


def bf(x):
    return np.asarray(x, np.float32).astype(BF16)


def f64(x):
    return np.asarray(x).astype(np.float64)


B, L, A, W = 128, 512, 2048, 8
EPS = 1e-8


def sigmoid(v):
    return 1.0 / (1.0 + np.exp(-v))


def setup_inputs():
    s, t = mx_kscale(L), mx_kscale(A)
    return {
        "z_current": bf(np.random.standard_normal((B, L)) * s),
        "z_window": bf(np.random.standard_normal((W, B, L)) * s),
        "Wq": bf(np.random.standard_normal((A, L)) / np.sqrt(L) / s),
        "Wk": bf(np.random.standard_normal((A, L)) / np.sqrt(L) / s),
        "Wv": bf(np.random.standard_normal((A, L)) / np.sqrt(L) / s * t[:, None]),
        "Wo": bf(np.random.standard_normal((L, A)) * 2.0 / np.sqrt(A) / t),
    }


def reference(z_current, z_window, Wq, Wk, Wv, Wo):
    sig_q = sigmoid(mxq(f64(z_current), 1, "e4m3") @ mxq(f64(Wq), 1, "e4m3").T)
    zw = mxq(f64(z_window), 2, "e4m3")
    k = zw @ mxq(f64(Wk), 1, "e4m3").T
    v = zw @ mxq(f64(Wv), 1, "e4m3").T
    m = k.max(axis=(1, 2), keepdims=True)
    e = np.exp(k - m)
    num = (e * v).sum(0)
    den = EPS + e.sum(0)
    h = sig_q * (num / den)
    return mxq(h, 1, "e4m3") @ mxq(f64(Wo), 1, "e4m3").T

@@ -1,0 +1,261 @@
+from contextlib import ExitStack
+
+import concourse.mybir as mybir
+from concourse.masks import make_identity
+
+F32 = mybir.dt.float32
+BF16 = mybir.dt.bfloat16
+U32 = mybir.dt.uint32
+U8 = mybir.dt.uint8
+FP8X4 = mybir.dt.float8_e4m3fn_x4
+ALU = mybir.AluOpType
+ACT = mybir.ActivationFunctionType
+AXIS_X = mybir.AxisListType.X
+
+P = 128
+L = 512
+A = 2048
+W = 8
+EPS = 1e-8
+CHUNK = 512
+CHUNKS = A // CHUNK
+BLOCKS = CHUNK // P
+WORDS = L // 2
+GROUP = 8
+RUN = 4
+GPSIMD_STEPS = 6
+
+FLOPS = 2 * P * L * A * (1 + 2 * W) + 2 * P * A * L
+
+
+def tile_aftblock_pa_kernel(tc, z_current, z_window, Wq, Wk, Wv, Wo, out):
+    nc = tc.nc
+    with ExitStack() as ctx:
+        ctx.enter_context(tc.manual_schedule())
+        keep = ctx.enter_context(tc.tile_pool(name="keep", bufs=1))
+        banks = ctx.enter_context(tc.psum_pool(name="banks", bufs=4))
+
+        ident = keep.tile([P, P], F32, name="ident")
+        make_identity(nc, ident[:])
+
+        z_codes = keep.tile([P, (W + 1) * P], U32, name="z_codes", align_bytes=64)
+        z_scales = keep.tile([P, (W + 1) * P], U8, name="z_scales", align_bytes=64)
+        wk_codes = keep.tile([P, A], U32, name="wk_codes", align_bytes=64)
+        wk_scales = keep.tile([P, A], U8, name="wk_scales", align_bytes=64)
+        wv_codes = keep.tile([P, A], U32, name="wv_codes", align_bytes=64)
+        wv_scales = keep.tile([P, A], U8, name="wv_scales", align_bytes=64)
+        wq_codes = keep.tile([P, A], U32, name="wq_codes", align_bytes=64)
+        wq_scales = keep.tile([P, A], U8, name="wq_scales", align_bytes=64)
+        wo_codes = keep.tile([P, CHUNKS * L], U32, name="wo_codes", align_bytes=64)
+        wo_scales = keep.tile([P, CHUNKS * L], U8, name="wo_scales", align_bytes=64)
+
+        k_sb = keep.tile([P, CHUNKS, W, CHUNK], F32, name="k_sb")
+        bank_max = keep.tile([P, CHUNKS, W], F32, name="bank_max")
+        row_max = keep.tile([P, W], F32, name="row_max")
+        neg_m = keep.tile([P, W], F32, name="neg_m")
+        gate = keep.tile([P, CHUNKS, P, BLOCKS], F32, name="gate")
+
+        def mx_pass(acc, lhs_codes, lhs_scales, lhs_cols, rhs_codes, rhs_scales, rhs_cols, start, stop):
+            nc.tensor.matmul_mx(
+                out=acc,
+                lhsT=lhs_codes[:, lhs_cols].bitcast(FP8X4),
+                lhsT_scale=lhs_scales[:, lhs_cols],
+                rhs=rhs_codes[:, rhs_cols].bitcast(FP8X4),
+                rhs_scale=rhs_scales[:, rhs_cols],
+                start=start,
+                stop=stop,
+            )
+
+        def step_cols(w):
+            return slice(w * P, (w + 1) * P)
+
+        def chunk_cols(c):
+            return slice(c * CHUNK, (c + 1) * CHUNK)
+
+        with tc.tile_pool(name="raw", bufs=1) as raw, tc.tile_pool(name="stage", bufs=3) as stage, tc.psum_pool(
+            name="flip", bufs=4
+        ) as flip:
+            z_raw = raw.tile([P, W + 1, L], BF16, name="z_raw")
+            nc.sync.dma_start(out=z_raw[:, 0:W, :], in_=z_window.rearrange("w b l -> b w l"))
+            nc.sync.dma_start(out=z_raw[:, W, :], in_=z_current)
+
+            def load_feature_rows(weight, name):
+                tile_ = raw.tile([P, A // P, L], BF16, name=name)
+                rows = weight.rearrange("(gu r e) l -> r gu (e l)", r=P, e=2)
+                for half in range(2):
+                    nc.sync.dma_start(
+                        out=tile_[:, GROUP * half : GROUP * (half + 1), :].rearrange("p (gu e) l -> p gu (e l)", e=2),
+                        in_=rows[:, GROUP // 2 * half : GROUP // 2 * (half + 1), :],
+                    )
+                return [tile_[:, j, :].bitcast(F32) for j in range(A // P)]
+
+            wk_blocks = load_feature_rows(Wk, "wk_raw")
+            wv_blocks = load_feature_rows(Wv, "wv_raw")
+            wq_blocks = load_feature_rows(Wq, "wq_raw")
+            wo_raw = raw.tile([P, L // P, A], BF16, name="wo_raw")
+            wo_rows = Wo.rearrange("(i p) a -> p i a", p=P)
+            for half in range(2):
+                cols = slice(A // 2 * half, A // 2 * (half + 1))
+                nc.sync.dma_start(out=wo_raw[:, :, cols], in_=wo_rows[:, :, cols])
+            wo_blocks = [
+                wo_raw[:, i, :].bitcast(F32)[:, WORDS * g : WORDS * (g + 1)]
+                for g in range(CHUNKS)
+                for i in range(L // P)
+            ]
+            z_blocks = [z_raw[:, s, :].bitcast(F32) for s in range(W + 1)]
+
+            def transpose_group(blocks, share_with_vector):
+                grouped = stage.tile([P, len(blocks) * P * BLOCKS], BF16, name="grouped", align_bytes=64)
+                words = grouped[:].bitcast(F32).rearrange("p (k r u) -> p k r u", r=P, u=2)
+                for first in range(0, len(blocks), 2):
+                    pair = blocks[first : first + 2]
+                    flipped = flip.tile([P, 2, 2, P], F32, name="flipped")
+                    for k, block in enumerate(pair):
+                        for u in range(2):
+                            nc.tensor.transpose(flipped[:, k, u, :], block[:, P * u : P * (u + 1)], ident[:])
+                    source = flipped[:, 0 : len(pair)].rearrange("p k u r -> p k r u")
+                    target = words[:, first : first + len(pair)]
+                    if share_with_vector and first % 4 == 2:
+                        nc.vector.tensor_copy(out=target, in_=source)
+                    else:
+                        nc.scalar.copy(out=target, in_=source)
+                return grouped
+
+            def quantise(grouped, codes, scales):
+                nc.vector.quantize_mx(out=codes.bitcast(FP8X4), scales=scales, in_=grouped[:])
+
+            def halves(blocks, codes, scales):
+                return [
+                    (blocks[GROUP * i : GROUP * (i + 1)], codes[:, GROUP * P * i : GROUP * P * (i + 1)],
+                     scales[:, GROUP * P * i : GROUP * P * (i + 1)])
+                    for i in range(2)
+                ]
+
+            window = transpose_group(z_blocks[0:W], True)
+            current = transpose_group(z_blocks[W:], True)
+            quantise(window, z_codes[:, 0 : W * P], z_scales[:, 0 : W * P])
+            quantise(current, z_codes[:, W * P :], z_scales[:, W * P :])
+            wk_halves = halves(wk_blocks, wk_codes, wk_scales)
+            first_half = transpose_group(wk_halves[0][0], True)
+            quantise(first_half, wk_halves[0][1], wk_halves[0][2])
+
+            later = (
+                wk_halves[1:]
+                + halves(wv_blocks, wv_codes, wv_scales)
+                + halves(wq_blocks, wq_codes, wq_scales)
+                + halves(wo_blocks, wo_codes, wo_scales)
+            )
+
+            def gate_stage():
+                for c in range(CHUNKS):
+                    q_ps = flip.tile([P, BLOCKS, P], F32, name="q_ps", tag="flipped")
+                    for t in range(BLOCKS):
+                        mx_pass(q_ps[:, t, :], wq_codes, wq_scales, step_cols(BLOCKS * c + t),
+                                z_codes, z_scales, step_cols(W), True, True)
+                    nc.scalar.activation(out=gate[:, c], in_=q_ps[:].rearrange("p t b -> p b t"), func=ACT.Exp, scale=-1.0)
+                flat = gate[:].rearrange("p c b t -> p (c b t)")
+                nc.gpsimd.tensor_scalar(out=flat, in0=flat, scalar1=1.0, scalar2=1.0, op0=ALU.add, op1=ALU.mult)
+
+            waiting = None
+            for round_ in range(CHUNKS * W // RUN):
+                for bank in range(RUN * round_, RUN * (round_ + 1)):
+                    c, w = divmod(bank, W)
+                    k_ps = banks.tile([P, CHUNK], F32, name="k_ps", tag="bank")
+                    mx_pass(k_ps[:], z_codes, z_scales, step_cols(w), wk_codes, wk_scales, chunk_cols(c), True, True)
+                    nc.vector.tensor_scalar(
+                        out=k_sb[:, c, w, :], in0=k_ps[:], scalar1=1.0, scalar2=None,
+                        op0=ALU.mult, op1=ALU.max, accum_out=bank_max[:, c, w : w + 1],
+                    )
+                if waiting is not None:
+                    quantise(*waiting)
+                    waiting = None
+                if round_ < len(later):
+                    blocks, codes, scales = later[round_]
+                    waiting = (transpose_group(blocks, False), codes, scales)
+                else:
+                    gate_stage()
+
+        nc.vector.tensor_reduce(out=row_max[:], in_=bank_max[:].rearrange("p c w -> p w c"), axis=AXIS_X, op=ALU.max)
+        for first in range(0, W, BLOCKS):
+            spread = banks.tile([P, BLOCKS, P], F32, name="spread", tag="bank")
+            for i in range(BLOCKS):
+                w = first + i
+                nc.tensor.transpose(spread[:, i, :], row_max[:, w : w + 1].to_broadcast([P, P]), ident[:])
+            nc.vector.tensor_reduce(out=neg_m[:, first : first + BLOCKS], in_=spread[:], axis=AXIS_X, op=ALU.max, negate=True)
+
+        with tc.tile_pool(name="prod", bufs=3 * RUN) as prod, tc.tile_pool(name="small", bufs=2) as small, tc.tile_pool(
+            name="late", bufs=1
+        ) as late, tc.psum_pool(name="sums", bufs=1) as sums:
+            divisor = late.tile([P, CHUNKS, P, BLOCKS], F32, name="divisor")
+            h_codes = late.tile([P, CHUNKS, P], U32, name="h_codes", align_bytes=64)
+            h_scales = late.tile([P, CHUNKS, P], U8, name="h_scales", align_bytes=64)
+            out_sb = late.tile([P, L], F32, name="out_sb")
+            products = {}
+            partial = {}
+            numerator = {}
+
+            def add_transposed(bank, source, first, last):
+                for t in range(BLOCKS):
+                    nc.tensor.matmul(
+                        out=bank[:, t, :], lhsT=source[:, P * t : P * (t + 1)], rhs=ident[:], is_transpose=True,
+                        start=first and t == 0, stop=last and t == BLOCKS - 1,
+                    )
+
+            def multiply(c, steps):
+                for w in steps:
+                    e = k_sb[:, c, w, :]
+                    v_ps = banks.tile([P, CHUNK], F32, name="v_ps", tag="bank")
+                    mx_pass(v_ps[:], z_codes, z_scales, step_cols(w), wv_codes, wv_scales, chunk_cols(c), True, True)
+                    nc.scalar.activation(out=e, in_=e, func=ACT.Exp, bias=neg_m[:, w : w + 1], scale=1.0)
+                    ev = prod.tile([P, CHUNK], F32, name="ev")
+                    nc.vector.tensor_tensor(out=ev[:], in0=e, in1=v_ps[:], op=ALU.mult)
+                    products[(c, w)] = ev
+                    if w == 1:
+                        partial[c] = small.tile([P, CHUNK], F32, name="partial")
+                        nc.gpsimd.tensor_tensor(out=partial[c][:], in0=k_sb[:, c, 0, :], in1=e, op=ALU.add)
+                    elif 1 < w < GPSIMD_STEPS:
+                        nc.gpsimd.tensor_tensor(out=partial[c][:], in0=partial[c][:], in1=e, op=ALU.add)
+
+            def sum_products(c, steps):
+                if c not in numerator:
+                    numerator[c] = sums.tile([P, BLOCKS, P], F32, name="numerator%d" % c)
+                for w in steps:
+                    add_transposed(numerator[c], products[(c, w)], w == 0, w == W - 1)
+
+            def sum_weights(c):
+                den_ps = banks.tile([P, BLOCKS, P], F32, name="den_ps", tag="bank")
+                add_transposed(den_ps, partial[c], True, False)
+                for w in range(GPSIMD_STEPS, W):
+                    add_transposed(den_ps, k_sb[:, c, w, :], False, w == W - 1)
+                nc.vector.scalar_tensor_tensor(
+                    out=divisor[:, c], in0=den_ps[:].rearrange("p t b -> p b t"), scalar=EPS, in1=gate[:, c],
+                    op0=ALU.add, op1=ALU.mult,
+                )
+
+            runs = [(c, range(first, first + RUN)) for c in range(CHUNKS) for first in range(0, W, RUN)]
+            for i, (c, steps) in enumerate(runs):
+                multiply(c, steps)
+                if i >= 1:
+                    sum_products(*runs[i - 1])
+                if i >= 2 and steps[0] == 0:
+                    sum_weights(c - 1)
+            sum_weights(CHUNKS - 1)
+            sum_products(*runs[-1])
+
+            for c in range(CHUNKS):
+                nc.scalar.activation(out=divisor[:, c], in_=divisor[:, c], func=ACT.Abs_reciprocal_sqrt)
+                nc.scalar.activation(out=divisor[:, c], in_=divisor[:, c], func=ACT.Square)
+                h = small.tile([P, P, BLOCKS], BF16, name="h", align_bytes=64)
+                nc.vector.tensor_tensor(out=h[:], in0=numerator[c][:].rearrange("p t b -> p b t"), in1=divisor[:, c], op=ALU.mult)
+                nc.vector.quantize_mx(out=h_codes[:, c, :].bitcast(FP8X4), scales=h_scales[:, c, :],
+                                      in_=h[:].rearrange("p b t -> p (b t)"))
+
+            out_ps = banks.tile([P, L], F32, name="out_ps", tag="bank")
+            for c in range(CHUNKS):
+                nc.tensor.matmul_mx(
+                    out=out_ps[:], lhsT=h_codes[:, c, :].bitcast(FP8X4), lhsT_scale=h_scales[:, c, :],
+                    rhs=wo_codes[:, chunk_cols(c)].bitcast(FP8X4), rhs_scale=wo_scales[:, chunk_cols(c)],
+                    start=c == 0, stop=c == CHUNKS - 1,
+                )
+            nc.scalar.copy(out=out_sb[:], in_=out_ps[:])
+            nc.sync.dma_start(out=out, in_=out_sb[:])

@@ -21,7 +21,8 @@ CHUNK = 512
 CHUNKS = A // CHUNK
 BLOCKS = CHUNK // P
 WORDS = L // 2
-GROUP = 8
+GROUP = 4
+ROUND = 2
 RUN = 4
 GPSIMD_STEPS = 6
 
@@ -72,37 +73,39 @@ def tile_aftblock_pa_kernel(tc, z_current, z_window, Wq, Wk, Wv, Wo, out):
         def chunk_cols(c):
             return slice(c * CHUNK, (c + 1) * CHUNK)
 
-        with tc.tile_pool(name="raw", bufs=1) as raw, tc.tile_pool(name="stage", bufs=3) as stage, tc.psum_pool(
+        with tc.tile_pool(name="raw", bufs=1) as raw, tc.tile_pool(name="stage", bufs=6) as stage, tc.psum_pool(
             name="flip", bufs=4
         ) as flip:
             z_raw = raw.tile([P, W + 1, L], BF16, name="z_raw")
-            nc.sync.dma_start(out=z_raw[:, 0:W, :], in_=z_window.rearrange("w b l -> b w l"))
-            nc.sync.dma_start(out=z_raw[:, W, :], in_=z_current)
-
-            def load_feature_rows(weight, name):
-                tile_ = raw.tile([P, A // P, L], BF16, name=name)
-                rows = weight.rearrange("(gu r e) l -> r gu (e l)", r=P, e=2)
-                for half in range(2):
-                    nc.sync.dma_start(
-                        out=tile_[:, GROUP * half : GROUP * (half + 1), :].rearrange("p (gu e) l -> p gu (e l)", e=2),
-                        in_=rows[:, GROUP // 2 * half : GROUP // 2 * (half + 1), :],
-                    )
-                return [tile_[:, j, :].bitcast(F32) for j in range(A // P)]
-
-            wk_blocks = load_feature_rows(Wk, "wk_raw")
-            wv_blocks = load_feature_rows(Wv, "wv_raw")
-            wq_blocks = load_feature_rows(Wq, "wq_raw")
+            wk_raw = raw.tile([P, A // P, L], BF16, name="wk_raw")
+            wv_raw = raw.tile([P, A // P, L], BF16, name="wv_raw")
+            wq_raw = raw.tile([P, A // P, L], BF16, name="wq_raw")
             wo_raw = raw.tile([P, L // P, A], BF16, name="wo_raw")
-            wo_rows = Wo.rearrange("(i p) a -> p i a", p=P)
-            for half in range(2):
-                cols = slice(A // 2 * half, A // 2 * (half + 1))
-                nc.sync.dma_start(out=wo_raw[:, :, cols], in_=wo_rows[:, :, cols])
-            wo_blocks = [
-                wo_raw[:, i, :].bitcast(F32)[:, WORDS * g : WORDS * (g + 1)]
-                for g in range(CHUNKS)
-                for i in range(L // P)
-            ]
-            z_blocks = [z_raw[:, s, :].bitcast(F32) for s in range(W + 1)]
+
+            def load_steps(first):
+                steps = slice(first, first + GROUP)
+                nc.sync.dma_start(out=z_raw[:, steps, :], in_=z_window[steps].rearrange("w b l -> b w l"))
+
+            def load_features(tile_, weight, c):
+                rows = weight.rearrange("(c u r e) l -> r c u (e l)", c=CHUNKS, u=2, e=2)
+                blocks = tile_[:, BLOCKS * c : BLOCKS * (c + 1), :]
+                nc.sync.dma_start(out=blocks.rearrange("p (u e) l -> p u (e l)", e=2), in_=rows[:, c])
+
+            def load_wo(g):
+                nc.sync.dma_start(out=wo_raw[:, :, chunk_cols(g)], in_=Wo.rearrange("(i p) a -> p i a", p=P)[:, :, chunk_cols(g)])
+
+            load_steps(0)
+            load_features(wk_raw, Wk, 0)
+            nc.sync.dma_start(out=z_raw[:, W, :], in_=z_current)
+            load_steps(GROUP)
+            for c in range(1, CHUNKS):
+                load_features(wk_raw, Wk, c)
+            for c in range(CHUNKS):
+                load_features(wv_raw, Wv, c)
+            for c in range(CHUNKS):
+                load_features(wq_raw, Wq, c)
+            for g in range(CHUNKS):
+                load_wo(g)
 
             def transpose_group(blocks, share_with_vector):
                 grouped = stage.tile([P, len(blocks) * P * BLOCKS], BF16, name="grouped", align_bytes=64)
@@ -115,7 +118,7 @@ def tile_aftblock_pa_kernel(tc, z_current, z_window, Wq, Wk, Wv, Wo, out):
                             nc.tensor.transpose(flipped[:, k, u, :], block[:, P * u : P * (u + 1)], ident[:])
                     source = flipped[:, 0 : len(pair)].rearrange("p k u r -> p k r u")
                     target = words[:, first : first + len(pair)]
-                    if share_with_vector and first % 4 == 2:
+                    if share_with_vector and first > 0:
                         nc.vector.tensor_copy(out=target, in_=source)
                     else:
                         nc.scalar.copy(out=target, in_=source)
@@ -124,27 +127,32 @@ def tile_aftblock_pa_kernel(tc, z_current, z_window, Wq, Wk, Wv, Wo, out):
             def quantise(grouped, codes, scales):
                 nc.vector.quantize_mx(out=codes.bitcast(FP8X4), scales=scales, in_=grouped[:])
 
-            def halves(blocks, codes, scales):
-                return [
-                    (blocks[GROUP * i : GROUP * (i + 1)], codes[:, GROUP * P * i : GROUP * P * (i + 1)],
-                     scales[:, GROUP * P * i : GROUP * P * (i + 1)])
-                    for i in range(2)
-                ]
+            def group_of(blocks, codes, scales, i):
+                cols = slice(GROUP * P * i, GROUP * P * (i + 1))
+                return blocks[GROUP * i : GROUP * (i + 1)], codes[:, cols], scales[:, cols]
 
-            window = transpose_group(z_blocks[0:W], True)
-            current = transpose_group(z_blocks[W:], True)
-            quantise(window, z_codes[:, 0 : W * P], z_scales[:, 0 : W * P])
-            quantise(current, z_codes[:, W * P :], z_scales[:, W * P :])
-            wk_halves = halves(wk_blocks, wk_codes, wk_scales)
-            first_half = transpose_group(wk_halves[0][0], True)
-            quantise(first_half, wk_halves[0][1], wk_halves[0][2])
+            z_blocks = [z_raw[:, s, :].bitcast(F32) for s in range(W + 1)]
+            wk_blocks = [wk_raw[:, j, :].bitcast(F32) for j in range(A // P)]
+            wv_blocks = [wv_raw[:, j, :].bitcast(F32) for j in range(A // P)]
+            wq_blocks = [wq_raw[:, j, :].bitcast(F32) for j in range(A // P)]
+            wo_blocks = [
+                wo_raw[:, i, :].bitcast(F32)[:, WORDS * g : WORDS * (g + 1)]
+                for g in range(CHUNKS)
+                for i in range(L // P)
+            ]
+
+            for blocks, codes, scales in (group_of(z_blocks, z_codes, z_scales, 0), group_of(wk_blocks, wk_codes, wk_scales, 0)):
+                quantise(transpose_group(blocks, True), codes, scales)
+            waiting = (transpose_group(z_blocks[W:], False), z_codes[:, W * P :], z_scales[:, W * P :])
 
             later = (
-                wk_halves[1:]
-                + halves(wv_blocks, wv_codes, wv_scales)
-                + halves(wq_blocks, wq_codes, wq_scales)
-                + halves(wo_blocks, wo_codes, wo_scales)
+                [group_of(z_blocks, z_codes, z_scales, 1)]
+                + [group_of(wk_blocks, wk_codes, wk_scales, c) for c in range(1, CHUNKS)]
+                + [group_of(wv_blocks, wv_codes, wv_scales, c) for c in range(CHUNKS)]
+                + [group_of(wq_blocks, wq_codes, wq_scales, c) for c in range(CHUNKS)]
             )
+            last = [group_of(wo_blocks, wo_codes, wo_scales, g) for g in range(CHUNKS)]
+            gate_round = len(later) + 2
 
             def gate_stage():
                 for c in range(CHUNKS):
@@ -156,9 +164,9 @@ def tile_aftblock_pa_kernel(tc, z_current, z_window, Wq, Wk, Wv, Wo, out):
                 flat = gate[:].rearrange("p c b t -> p (c b t)")
                 nc.gpsimd.tensor_scalar(out=flat, in0=flat, scalar1=1.0, scalar2=1.0, op0=ALU.add, op1=ALU.mult)
 
-            waiting = None
-            for round_ in range(CHUNKS * W // RUN):
-                for bank in range(RUN * round_, RUN * (round_ + 1)):
+            wo_grouped = []
+            for round_ in range(CHUNKS * W // ROUND):
+                for bank in range(ROUND * round_, ROUND * (round_ + 1)):
                     c, w = divmod(bank, W)
                     k_ps = banks.tile([P, CHUNK], F32, name="k_ps", tag="bank")
                     mx_pass(k_ps[:], z_codes, z_scales, step_cols(w), wk_codes, wk_scales, chunk_cols(c), True, True)
@@ -173,15 +181,26 @@ def tile_aftblock_pa_kernel(tc, z_current, z_window, Wq, Wk, Wv, Wo, out):
                     blocks, codes, scales = later[round_]
                     waiting = (transpose_group(blocks, False), codes, scales)
                 else:
+                    wo_grouped.append(transpose_group(last[round_ - len(later)][0], False))
+                if round_ == gate_round:
                     gate_stage()
 
-        nc.vector.tensor_reduce(out=row_max[:], in_=bank_max[:].rearrange("p c w -> p w c"), axis=AXIS_X, op=ALU.max)
-        for first in range(0, W, BLOCKS):
-            spread = banks.tile([P, BLOCKS, P], F32, name="spread", tag="bank")
-            for i in range(BLOCKS):
-                w = first + i
-                nc.tensor.transpose(spread[:, i, :], row_max[:, w : w + 1].to_broadcast([P, P]), ident[:])
-            nc.vector.tensor_reduce(out=neg_m[:, first : first + BLOCKS], in_=spread[:], axis=AXIS_X, op=ALU.max, negate=True)
+            nc.vector.tensor_reduce(out=row_max[:], in_=bank_max[:].rearrange("p c w -> p w c"), axis=AXIS_X, op=ALU.max)
+            spreads = []
+            for first in range(0, W, BLOCKS):
+                spread = banks.tile([P, BLOCKS, P], F32, name="spread", tag="bank")
+                for i in range(BLOCKS):
+                    w = first + i
+                    nc.tensor.transpose(spread[:, i, :], row_max[:, w : w + 1].to_broadcast([P, P]), ident[:])
+                spreads.append(spread)
+            for g in range(0, CHUNKS // 2):
+                quantise(wo_grouped[g], last[g][1], last[g][2])
+            for i, spread in enumerate(spreads):
+                nc.vector.tensor_reduce(
+                    out=neg_m[:, BLOCKS * i : BLOCKS * (i + 1)], in_=spread[:], axis=AXIS_X, op=ALU.max, negate=True
+                )
+            for g in range(CHUNKS // 2, CHUNKS):
+                quantise(wo_grouped[g], last[g][1], last[g][2])
 
         with tc.tile_pool(name="prod", bufs=3 * RUN) as prod, tc.tile_pool(name="small", bufs=2) as small, tc.tile_pool(
             name="late", bufs=1

@@ -34,6 +34,7 @@ def tile_aftblock_pa_kernel(tc, z_current, z_window, Wq, Wk, Wv, Wo, out):
     with ExitStack() as ctx:
         ctx.enter_context(tc.manual_schedule())
         keep = ctx.enter_context(tc.tile_pool(name="keep", bufs=1))
+        stage = ctx.enter_context(tc.tile_pool(name="stage", bufs=6))
         banks = ctx.enter_context(tc.psum_pool(name="banks", bufs=4))
 
         ident = keep.tile([P, P], F32, name="ident")
@@ -73,9 +74,7 @@ def tile_aftblock_pa_kernel(tc, z_current, z_window, Wq, Wk, Wv, Wo, out):
         def chunk_cols(c):
             return slice(c * CHUNK, (c + 1) * CHUNK)
 
-        with tc.tile_pool(name="raw", bufs=1) as raw, tc.tile_pool(name="stage", bufs=6) as stage, tc.psum_pool(
-            name="flip", bufs=4
-        ) as flip:
+        with tc.tile_pool(name="raw", bufs=1) as raw, tc.psum_pool(name="flip", bufs=4) as flip:
             z_raw = raw.tile([P, W + 1, L], BF16, name="z_raw")
             wk_raw = raw.tile([P, A // P, L], BF16, name="wk_raw")
             wv_raw = raw.tile([P, A // P, L], BF16, name="wv_raw")
@@ -101,9 +100,9 @@ def tile_aftblock_pa_kernel(tc, z_current, z_window, Wq, Wk, Wv, Wo, out):
             for c in range(1, CHUNKS):
                 load_features(wk_raw, Wk, c)
             for c in range(CHUNKS):
-                load_features(wv_raw, Wv, c)
-            for c in range(CHUNKS):
                 load_features(wq_raw, Wq, c)
+            for c in range(CHUNKS):
+                load_features(wv_raw, Wv, c)
             for g in range(CHUNKS):
                 load_wo(g)
 
@@ -148,11 +147,11 @@ def tile_aftblock_pa_kernel(tc, z_current, z_window, Wq, Wk, Wv, Wo, out):
             later = (
                 [group_of(z_blocks, z_codes, z_scales, 1)]
                 + [group_of(wk_blocks, wk_codes, wk_scales, c) for c in range(1, CHUNKS)]
-                + [group_of(wv_blocks, wv_codes, wv_scales, c) for c in range(CHUNKS)]
                 + [group_of(wq_blocks, wq_codes, wq_scales, c) for c in range(CHUNKS)]
+                + [group_of(wv_blocks, wv_codes, wv_scales, c) for c in range(CHUNKS)]
             )
             last = [group_of(wo_blocks, wo_codes, wo_scales, g) for g in range(CHUNKS)]
-            gate_round = len(later) + 2
+            gate_round = len(later) - CHUNKS + 2
 
             def gate_stage():
                 for c in range(CHUNKS):
@@ -164,8 +163,26 @@ def tile_aftblock_pa_kernel(tc, z_current, z_window, Wq, Wk, Wv, Wo, out):
                 flat = gate[:].rearrange("p c b t -> p (c b t)")
                 nc.gpsimd.tensor_scalar(out=flat, in0=flat, scalar1=1.0, scalar2=1.0, op0=ALU.add, op1=ALU.mult)
 
+            def row_maxima(first):
+                steps = slice(first, first + BLOCKS)
+                nc.vector.tensor_reduce(
+                    out=row_max[:, steps], in_=bank_max[:, :, steps].rearrange("p c w -> p w c"), axis=AXIS_X, op=ALU.max
+                )
+
+            def spread_maxima(first):
+                spread = banks.tile([P, BLOCKS, P], F32, name="spread", tag="bank")
+                for i in range(BLOCKS):
+                    nc.tensor.transpose(spread[:, i, :], row_max[:, first + i : first + i + 1].to_broadcast([P, P]), ident[:])
+                return spread
+
+            def negated_maximum(spread, first):
+                nc.vector.tensor_reduce(out=neg_m[:, first : first + BLOCKS], in_=spread[:], axis=AXIS_X, op=ALU.max, negate=True)
+
+            first_steps = 0
+            last_steps = BLOCKS
             wo_grouped = []
-            for round_ in range(CHUNKS * W // ROUND):
+            rounds = CHUNKS * W // ROUND
+            for round_ in range(rounds):
                 for bank in range(ROUND * round_, ROUND * (round_ + 1)):
                     c, w = divmod(bank, W)
                     k_ps = banks.tile([P, CHUNK], F32, name="k_ps", tag="bank")
@@ -184,23 +201,17 @@ def tile_aftblock_pa_kernel(tc, z_current, z_window, Wq, Wk, Wv, Wo, out):
                     wo_grouped.append(transpose_group(last[round_ - len(later)][0], False))
                 if round_ == gate_round:
                     gate_stage()
+                if round_ == rounds - 3:
+                    row_maxima(first_steps)
+                if round_ == rounds - 2:
+                    spread_first = spread_maxima(first_steps)
+                if round_ == rounds - 1:
+                    negated_maximum(spread_first, first_steps)
 
-            nc.vector.tensor_reduce(out=row_max[:], in_=bank_max[:].rearrange("p c w -> p w c"), axis=AXIS_X, op=ALU.max)
-            spreads = []
-            for first in range(0, W, BLOCKS):
-                spread = banks.tile([P, BLOCKS, P], F32, name="spread", tag="bank")
-                for i in range(BLOCKS):
-                    w = first + i
-                    nc.tensor.transpose(spread[:, i, :], row_max[:, w : w + 1].to_broadcast([P, P]), ident[:])
-                spreads.append(spread)
-            for g in range(0, CHUNKS // 2):
-                quantise(wo_grouped[g], last[g][1], last[g][2])
-            for i, spread in enumerate(spreads):
-                nc.vector.tensor_reduce(
-                    out=neg_m[:, BLOCKS * i : BLOCKS * (i + 1)], in_=spread[:], axis=AXIS_X, op=ALU.max, negate=True
-                )
-            for g in range(CHUNKS // 2, CHUNKS):
-                quantise(wo_grouped[g], last[g][1], last[g][2])
+            row_maxima(last_steps)
+            spread_last = spread_maxima(last_steps)
+            quantise(wo_grouped[0], last[0][1], last[0][2])
+            negated_maximum(spread_last, last_steps)
 
         with tc.tile_pool(name="prod", bufs=3 * RUN) as prod, tc.tile_pool(name="small", bufs=2) as small, tc.tile_pool(
             name="late", bufs=1
@@ -209,9 +220,18 @@ def tile_aftblock_pa_kernel(tc, z_current, z_window, Wq, Wk, Wv, Wo, out):
             h_codes = late.tile([P, CHUNKS, P], U32, name="h_codes", align_bytes=64)
             h_scales = late.tile([P, CHUNKS, P], U8, name="h_scales", align_bytes=64)
             out_sb = late.tile([P, L], F32, name="out_sb")
+            partial = late.tile([P, CHUNKS, CHUNK], F32, name="partial")
             products = {}
-            partial = {}
             numerator = {}
+
+            for c in range(CHUNKS):
+                for w in range(W):
+                    e = k_sb[:, c, w, :]
+                    nc.scalar.activation(out=e, in_=e, func=ACT.Exp, bias=neg_m[:, w : w + 1], scale=1.0)
+                    if w == 1:
+                        nc.gpsimd.tensor_tensor(out=partial[:, c, :], in0=k_sb[:, c, 0, :], in1=e, op=ALU.add)
+                    elif 1 < w < GPSIMD_STEPS:
+                        nc.gpsimd.tensor_tensor(out=partial[:, c, :], in0=partial[:, c, :], in1=e, op=ALU.add)
 
             def add_transposed(bank, source, first, last):
                 for t in range(BLOCKS):
@@ -222,18 +242,11 @@ def tile_aftblock_pa_kernel(tc, z_current, z_window, Wq, Wk, Wv, Wo, out):
 
             def multiply(c, steps):
                 for w in steps:
-                    e = k_sb[:, c, w, :]
                     v_ps = banks.tile([P, CHUNK], F32, name="v_ps", tag="bank")
                     mx_pass(v_ps[:], z_codes, z_scales, step_cols(w), wv_codes, wv_scales, chunk_cols(c), True, True)
-                    nc.scalar.activation(out=e, in_=e, func=ACT.Exp, bias=neg_m[:, w : w + 1], scale=1.0)
                     ev = prod.tile([P, CHUNK], F32, name="ev")
-                    nc.vector.tensor_tensor(out=ev[:], in0=e, in1=v_ps[:], op=ALU.mult)
+                    nc.vector.tensor_tensor(out=ev[:], in0=k_sb[:, c, w, :], in1=v_ps[:], op=ALU.mult)
                     products[(c, w)] = ev
-                    if w == 1:
-                        partial[c] = small.tile([P, CHUNK], F32, name="partial")
-                        nc.gpsimd.tensor_tensor(out=partial[c][:], in0=k_sb[:, c, 0, :], in1=e, op=ALU.add)
-                    elif 1 < w < GPSIMD_STEPS:
-                        nc.gpsimd.tensor_tensor(out=partial[c][:], in0=partial[c][:], in1=e, op=ALU.add)
 
             def sum_products(c, steps):
                 if c not in numerator:
@@ -241,33 +254,38 @@ def tile_aftblock_pa_kernel(tc, z_current, z_window, Wq, Wk, Wv, Wo, out):
                 for w in steps:
                     add_transposed(numerator[c], products[(c, w)], w == 0, w == W - 1)
 
-            def sum_weights(c):
+            def reciprocal_divisor(c):
                 den_ps = banks.tile([P, BLOCKS, P], F32, name="den_ps", tag="bank")
-                add_transposed(den_ps, partial[c], True, False)
+                add_transposed(den_ps, partial[:, c, :], True, False)
                 for w in range(GPSIMD_STEPS, W):
                     add_transposed(den_ps, k_sb[:, c, w, :], False, w == W - 1)
                 nc.vector.scalar_tensor_tensor(
                     out=divisor[:, c], in0=den_ps[:].rearrange("p t b -> p b t"), scalar=EPS, in1=gate[:, c],
                     op0=ALU.add, op1=ALU.mult,
                 )
-
-            runs = [(c, range(first, first + RUN)) for c in range(CHUNKS) for first in range(0, W, RUN)]
-            for i, (c, steps) in enumerate(runs):
-                multiply(c, steps)
-                if i >= 1:
-                    sum_products(*runs[i - 1])
-                if i >= 2 and steps[0] == 0:
-                    sum_weights(c - 1)
-            sum_weights(CHUNKS - 1)
-            sum_products(*runs[-1])
-
-            for c in range(CHUNKS):
                 nc.scalar.activation(out=divisor[:, c], in_=divisor[:, c], func=ACT.Abs_reciprocal_sqrt)
                 nc.scalar.activation(out=divisor[:, c], in_=divisor[:, c], func=ACT.Square)
+
+            def hidden(c):
                 h = small.tile([P, P, BLOCKS], BF16, name="h", align_bytes=64)
                 nc.vector.tensor_tensor(out=h[:], in0=numerator[c][:].rearrange("p t b -> p b t"), in1=divisor[:, c], op=ALU.mult)
                 nc.vector.quantize_mx(out=h_codes[:, c, :].bitcast(FP8X4), scales=h_scales[:, c, :],
                                       in_=h[:].rearrange("p b t -> p (b t)"))
+
+            runs = [(c, range(first, first + RUN)) for c in range(CHUNKS) for first in range(0, W, RUN)]
+            for i, (c, steps) in enumerate(runs):
+                multiply(c, steps)
+                if i + 1 < CHUNKS:
+                    quantise(wo_grouped[i + 1], last[i + 1][1], last[i + 1][2])
+                if i >= 1:
+                    sum_products(*runs[i - 1])
+                if steps[0] == 0 and c >= 1:
+                    reciprocal_divisor(c - 1)
+                if i > len(runs) - CHUNKS:
+                    hidden(i - len(runs) + CHUNKS - 1)
+            reciprocal_divisor(CHUNKS - 1)
+            sum_products(*runs[-1])
+            hidden(CHUNKS - 1)
 
             out_ps = banks.tile([P, L], F32, name="out_ps", tag="bank")
             for c in range(CHUNKS):

from contextlib import ExitStack

import concourse.mybir as mybir
from concourse.masks import make_identity

F32 = mybir.dt.float32
BF16 = mybir.dt.bfloat16
U32 = mybir.dt.uint32
U8 = mybir.dt.uint8
FP8X4 = mybir.dt.float8_e4m3fn_x4
ALU = mybir.AluOpType
ACT = mybir.ActivationFunctionType
AXIS_X = mybir.AxisListType.X

P = 128
L = 512
A = 2048
W = 8
EPS = 1e-8
CHUNK = 512
CHUNKS = A // CHUNK
BLOCKS = CHUNK // P
WORDS = L // 2
GROUP = 4
ROUND = 2
RUN = 4
GPSIMD_STEPS = 6

FLOPS = 2 * P * L * A * (1 + 2 * W) + 2 * P * A * L


def tile_aftblock_pa_kernel(tc, z_current, z_window, Wq, Wk, Wv, Wo, out):
    nc = tc.nc
    with ExitStack() as ctx:
        ctx.enter_context(tc.manual_schedule())
        keep = ctx.enter_context(tc.tile_pool(name="keep", bufs=1))
        stage = ctx.enter_context(tc.tile_pool(name="stage", bufs=6))
        banks = ctx.enter_context(tc.psum_pool(name="banks", bufs=4))

        ident = keep.tile([P, P], F32, name="ident")
        make_identity(nc, ident[:])

        z_codes = keep.tile([P, (W + 1) * P], U32, name="z_codes", align_bytes=64)
        z_scales = keep.tile([P, (W + 1) * P], U8, name="z_scales", align_bytes=64)
        wk_codes = keep.tile([P, A], U32, name="wk_codes", align_bytes=64)
        wk_scales = keep.tile([P, A], U8, name="wk_scales", align_bytes=64)
        wv_codes = keep.tile([P, A], U32, name="wv_codes", align_bytes=64)
        wv_scales = keep.tile([P, A], U8, name="wv_scales", align_bytes=64)
        wq_codes = keep.tile([P, A], U32, name="wq_codes", align_bytes=64)
        wq_scales = keep.tile([P, A], U8, name="wq_scales", align_bytes=64)
        wo_codes = keep.tile([P, CHUNKS * L], U32, name="wo_codes", align_bytes=64)
        wo_scales = keep.tile([P, CHUNKS * L], U8, name="wo_scales", align_bytes=64)

        k_sb = keep.tile([P, CHUNKS, W, CHUNK], F32, name="k_sb")
        bank_max = keep.tile([P, CHUNKS, W], F32, name="bank_max")
        row_max = keep.tile([P, W], F32, name="row_max")
        neg_m = keep.tile([P, W], F32, name="neg_m")
        gate = keep.tile([P, CHUNKS, P, BLOCKS], F32, name="gate")

        def mx_pass(acc, lhs_codes, lhs_scales, lhs_cols, rhs_codes, rhs_scales, rhs_cols, start, stop):
            nc.tensor.matmul_mx(
                out=acc,
                lhsT=lhs_codes[:, lhs_cols].bitcast(FP8X4),
                lhsT_scale=lhs_scales[:, lhs_cols],
                rhs=rhs_codes[:, rhs_cols].bitcast(FP8X4),
                rhs_scale=rhs_scales[:, rhs_cols],
                start=start,
                stop=stop,
            )

        def step_cols(w):
            return slice(w * P, (w + 1) * P)

        def chunk_cols(c):
            return slice(c * CHUNK, (c + 1) * CHUNK)

        with tc.tile_pool(name="raw", bufs=1) as raw, tc.psum_pool(name="flip", bufs=4) as flip:
            z_raw = raw.tile([P, W + 1, L], BF16, name="z_raw")
            wk_raw = raw.tile([P, A // P, L], BF16, name="wk_raw")
            wv_raw = raw.tile([P, A // P, L], BF16, name="wv_raw")
            wq_raw = raw.tile([P, A // P, L], BF16, name="wq_raw")
            wo_raw = raw.tile([P, L // P, A], BF16, name="wo_raw")

            def load_steps(first):
                steps = slice(first, first + GROUP)
                nc.sync.dma_start(out=z_raw[:, steps, :], in_=z_window[steps].rearrange("w b l -> b w l"))

            def load_features(tile_, weight, c):
                rows = weight.rearrange("(c u r e) l -> r c u (e l)", c=CHUNKS, u=2, e=2)
                blocks = tile_[:, BLOCKS * c : BLOCKS * (c + 1), :]
                nc.sync.dma_start(out=blocks.rearrange("p (u e) l -> p u (e l)", e=2), in_=rows[:, c])

            def load_wo(g):
                nc.sync.dma_start(out=wo_raw[:, :, chunk_cols(g)], in_=Wo.rearrange("(i p) a -> p i a", p=P)[:, :, chunk_cols(g)])

            load_steps(0)
            load_features(wk_raw, Wk, 0)
            nc.sync.dma_start(out=z_raw[:, W, :], in_=z_current)
            load_steps(GROUP)
            for c in range(1, CHUNKS):
                load_features(wk_raw, Wk, c)
            for c in range(CHUNKS):
                load_features(wq_raw, Wq, c)
            for c in range(CHUNKS):
                load_features(wv_raw, Wv, c)
            for g in range(CHUNKS):
                load_wo(g)

            def transpose_group(blocks, share_with_vector):
                grouped = stage.tile([P, len(blocks) * P * BLOCKS], BF16, name="grouped", align_bytes=64)
                words = grouped[:].bitcast(F32).rearrange("p (k r u) -> p k r u", r=P, u=2)
                for first in range(0, len(blocks), 2):
                    pair = blocks[first : first + 2]
                    flipped = flip.tile([P, 2, 2, P], F32, name="flipped")
                    for k, block in enumerate(pair):
                        for u in range(2):
                            nc.tensor.transpose(flipped[:, k, u, :], block[:, P * u : P * (u + 1)], ident[:])
                    source = flipped[:, 0 : len(pair)].rearrange("p k u r -> p k r u")
                    target = words[:, first : first + len(pair)]
                    if share_with_vector and first > 0:
                        nc.vector.tensor_copy(out=target, in_=source)
                    else:
                        nc.scalar.copy(out=target, in_=source)
                return grouped

            def quantise(grouped, codes, scales):
                nc.vector.quantize_mx(out=codes.bitcast(FP8X4), scales=scales, in_=grouped[:])

            def group_of(blocks, codes, scales, i):
                cols = slice(GROUP * P * i, GROUP * P * (i + 1))
                return blocks[GROUP * i : GROUP * (i + 1)], codes[:, cols], scales[:, cols]

            z_blocks = [z_raw[:, s, :].bitcast(F32) for s in range(W + 1)]
            wk_blocks = [wk_raw[:, j, :].bitcast(F32) for j in range(A // P)]
            wv_blocks = [wv_raw[:, j, :].bitcast(F32) for j in range(A // P)]
            wq_blocks = [wq_raw[:, j, :].bitcast(F32) for j in range(A // P)]
            wo_blocks = [
                wo_raw[:, i, :].bitcast(F32)[:, WORDS * g : WORDS * (g + 1)]
                for g in range(CHUNKS)
                for i in range(L // P)
            ]

            for blocks, codes, scales in (group_of(z_blocks, z_codes, z_scales, 0), group_of(wk_blocks, wk_codes, wk_scales, 0)):
                quantise(transpose_group(blocks, True), codes, scales)
            waiting = (transpose_group(z_blocks[W:], False), z_codes[:, W * P :], z_scales[:, W * P :])

            later = (
                [group_of(z_blocks, z_codes, z_scales, 1)]
                + [group_of(wk_blocks, wk_codes, wk_scales, c) for c in range(1, CHUNKS)]
                + [group_of(wq_blocks, wq_codes, wq_scales, c) for c in range(CHUNKS)]
                + [group_of(wv_blocks, wv_codes, wv_scales, c) for c in range(CHUNKS)]
            )
            last = [group_of(wo_blocks, wo_codes, wo_scales, g) for g in range(CHUNKS)]
            gate_round = len(later) - CHUNKS + 2

            def gate_stage():
                for c in range(CHUNKS):
                    q_ps = flip.tile([P, BLOCKS, P], F32, name="q_ps", tag="flipped")
                    for t in range(BLOCKS):
                        mx_pass(q_ps[:, t, :], wq_codes, wq_scales, step_cols(BLOCKS * c + t),
                                z_codes, z_scales, step_cols(W), True, True)
                    nc.scalar.activation(out=gate[:, c], in_=q_ps[:].rearrange("p t b -> p b t"), func=ACT.Exp, scale=-1.0)
                flat = gate[:].rearrange("p c b t -> p (c b t)")
                nc.gpsimd.tensor_scalar(out=flat, in0=flat, scalar1=1.0, scalar2=1.0, op0=ALU.add, op1=ALU.mult)

            def row_maxima(first):
                steps = slice(first, first + BLOCKS)
                nc.vector.tensor_reduce(
                    out=row_max[:, steps], in_=bank_max[:, :, steps].rearrange("p c w -> p w c"), axis=AXIS_X, op=ALU.max
                )

            def spread_maxima(first):
                spread = banks.tile([P, BLOCKS, P], F32, name="spread", tag="bank")
                for i in range(BLOCKS):
                    nc.tensor.transpose(spread[:, i, :], row_max[:, first + i : first + i + 1].to_broadcast([P, P]), ident[:])
                return spread

            def negated_maximum(spread, first):
                nc.vector.tensor_reduce(out=neg_m[:, first : first + BLOCKS], in_=spread[:], axis=AXIS_X, op=ALU.max, negate=True)

            first_steps = 0
            last_steps = BLOCKS
            wo_grouped = []
            rounds = CHUNKS * W // ROUND
            for round_ in range(rounds):
                for bank in range(ROUND * round_, ROUND * (round_ + 1)):
                    c, w = divmod(bank, W)
                    k_ps = banks.tile([P, CHUNK], F32, name="k_ps", tag="bank")
                    mx_pass(k_ps[:], z_codes, z_scales, step_cols(w), wk_codes, wk_scales, chunk_cols(c), True, True)
                    nc.vector.tensor_scalar(
                        out=k_sb[:, c, w, :], in0=k_ps[:], scalar1=1.0, scalar2=None,
                        op0=ALU.mult, op1=ALU.max, accum_out=bank_max[:, c, w : w + 1],
                    )
                if waiting is not None:
                    quantise(*waiting)
                    waiting = None
                if round_ < len(later):
                    blocks, codes, scales = later[round_]
                    waiting = (transpose_group(blocks, False), codes, scales)
                else:
                    wo_grouped.append(transpose_group(last[round_ - len(later)][0], False))
                if round_ == gate_round:
                    gate_stage()
                if round_ == rounds - 3:
                    row_maxima(first_steps)
                if round_ == rounds - 2:
                    spread_first = spread_maxima(first_steps)
                if round_ == rounds - 1:
                    negated_maximum(spread_first, first_steps)

            row_maxima(last_steps)
            spread_last = spread_maxima(last_steps)
            quantise(wo_grouped[0], last[0][1], last[0][2])
            negated_maximum(spread_last, last_steps)

        with tc.tile_pool(name="prod", bufs=3 * RUN) as prod, tc.tile_pool(name="small", bufs=2) as small, tc.tile_pool(
            name="late", bufs=1
        ) as late, tc.psum_pool(name="sums", bufs=1) as sums:
            divisor = late.tile([P, CHUNKS, P, BLOCKS], F32, name="divisor")
            h_codes = late.tile([P, CHUNKS, P], U32, name="h_codes", align_bytes=64)
            h_scales = late.tile([P, CHUNKS, P], U8, name="h_scales", align_bytes=64)
            out_sb = late.tile([P, L], F32, name="out_sb")
            partial = late.tile([P, CHUNKS, CHUNK], F32, name="partial")
            products = {}
            numerator = {}

            for c in range(CHUNKS):
                for w in range(W):
                    e = k_sb[:, c, w, :]
                    nc.scalar.activation(out=e, in_=e, func=ACT.Exp, bias=neg_m[:, w : w + 1], scale=1.0)
                    if w == 1:
                        nc.gpsimd.tensor_tensor(out=partial[:, c, :], in0=k_sb[:, c, 0, :], in1=e, op=ALU.add)
                    elif 1 < w < GPSIMD_STEPS:
                        nc.gpsimd.tensor_tensor(out=partial[:, c, :], in0=partial[:, c, :], in1=e, op=ALU.add)

            def add_transposed(bank, source, first, last):
                for t in range(BLOCKS):
                    nc.tensor.matmul(
                        out=bank[:, t, :], lhsT=source[:, P * t : P * (t + 1)], rhs=ident[:], is_transpose=True,
                        start=first and t == 0, stop=last and t == BLOCKS - 1,
                    )

            def multiply(c, steps):
                for w in steps:
                    v_ps = banks.tile([P, CHUNK], F32, name="v_ps", tag="bank")
                    mx_pass(v_ps[:], z_codes, z_scales, step_cols(w), wv_codes, wv_scales, chunk_cols(c), True, True)
                    ev = prod.tile([P, CHUNK], F32, name="ev")
                    nc.vector.tensor_tensor(out=ev[:], in0=k_sb[:, c, w, :], in1=v_ps[:], op=ALU.mult)
                    products[(c, w)] = ev

            def sum_products(c, steps):
                if c not in numerator:
                    numerator[c] = sums.tile([P, BLOCKS, P], F32, name="numerator%d" % c)
                for w in steps:
                    add_transposed(numerator[c], products[(c, w)], w == 0, w == W - 1)

            def reciprocal_divisor(c):
                den_ps = banks.tile([P, BLOCKS, P], F32, name="den_ps", tag="bank")
                add_transposed(den_ps, partial[:, c, :], True, False)
                for w in range(GPSIMD_STEPS, W):
                    add_transposed(den_ps, k_sb[:, c, w, :], False, w == W - 1)
                nc.vector.scalar_tensor_tensor(
                    out=divisor[:, c], in0=den_ps[:].rearrange("p t b -> p b t"), scalar=EPS, in1=gate[:, c],
                    op0=ALU.add, op1=ALU.mult,
                )
                nc.scalar.activation(out=divisor[:, c], in_=divisor[:, c], func=ACT.Abs_reciprocal_sqrt)
                nc.scalar.activation(out=divisor[:, c], in_=divisor[:, c], func=ACT.Square)

            def hidden(c):
                h = small.tile([P, P, BLOCKS], BF16, name="h", align_bytes=64)
                nc.vector.tensor_tensor(out=h[:], in0=numerator[c][:].rearrange("p t b -> p b t"), in1=divisor[:, c], op=ALU.mult)
                nc.vector.quantize_mx(out=h_codes[:, c, :].bitcast(FP8X4), scales=h_scales[:, c, :],
                                      in_=h[:].rearrange("p b t -> p (b t)"))

            runs = [(c, range(first, first + RUN)) for c in range(CHUNKS) for first in range(0, W, RUN)]
            for i, (c, steps) in enumerate(runs):
                multiply(c, steps)
                if i + 1 < CHUNKS:
                    quantise(wo_grouped[i + 1], last[i + 1][1], last[i + 1][2])
                if i >= 1:
                    sum_products(*runs[i - 1])
                if steps[0] == 0 and c >= 1:
                    reciprocal_divisor(c - 1)
                if i > len(runs) - CHUNKS:
                    hidden(i - len(runs) + CHUNKS - 1)
            reciprocal_divisor(CHUNKS - 1)
            sum_products(*runs[-1])
            hidden(CHUNKS - 1)

            out_ps = banks.tile([P, L], F32, name="out_ps", tag="bank")
            for c in range(CHUNKS):
                nc.tensor.matmul_mx(
                    out=out_ps[:], lhsT=h_codes[:, c, :].bitcast(FP8X4), lhsT_scale=h_scales[:, c, :],
                    rhs=wo_codes[:, chunk_cols(c)].bitcast(FP8X4), rhs_scale=wo_scales[:, chunk_cols(c)],
                    start=c == 0, stop=c == CHUNKS - 1,
                )
            nc.scalar.copy(out=out_sb[:], in_=out_ps[:])
            nc.sync.dma_start(out=out, in_=out_sb[:])
